import numpy as np
import ml_dtypes


def mxq(x, axis, fmt="e4m3"):
    dtype, down = {"e4m3": (ml_dtypes.float8_e4m3fn, 7), "e5m2": (ml_dtypes.float8_e5m2, 14)}[fmt]
    v = np.moveaxis(np.asarray(x, np.float32).astype(ml_dtypes.bfloat16).astype(np.float64), axis, -1)
    blocks = v.reshape(v.shape[:-1] + (-1, 32))
    amax = np.abs(blocks).max(-1, keepdims=True)
    byte = np.maximum(np.where(amax > 0, np.frexp(amax)[1] - 1 + 127, 0) - down, 1)
    scale = np.exp2(byte - 127.0)
    codes = (blocks / scale).astype(np.float32).astype(dtype).astype(np.float64)
    return np.moveaxis((codes * scale).reshape(v.shape), -1, axis)


WIDE = False


def mx_kscale(k):
    if not WIDE:
        return np.ones(k)
    levels = np.array([10, -10, 5, -5, 0])
    if k % 512:
        return np.exp2(np.random.permutation(np.resize(levels, k // 32))).repeat(32)
    a = np.empty((k // 512, 16))
    for p in range(k // 512):
        a[p, :8] = np.random.permutation(np.resize(levels, 8))
        for g in range(8):
            far = levels[np.abs(levels - a[p, g]) >= 10]
            a[p, g + 8] = far[np.random.randint(len(far))]
    return np.exp2(a.ravel()).repeat(32)


BF16 = ml_dtypes.bfloat16


def bf(x):
    return np.asarray(x, np.float32).astype(BF16)


def f64(x):
    return np.asarray(x).astype(np.float64)


B, D, S, N = 1024, 2048, 4, 128
DS = D // S


def sigmoid(v):
    return 1.0 / (1.0 + np.exp(-v))


def draw0():
    s = mx_kscale(D)
    t = np.maximum(1.0 + 2.0 * np.random.standard_normal((B, N, S)), 0.0) + np.maximum(1.0 + 2.0 * np.random.standard_normal((B, N, S)), 0.0)
    return {"a": bf(t * t / (t * t).sum(axis=1, keepdims=True)),
            "vr": bf(np.random.standard_normal((N, S, DS)) * 0.5 * np.sqrt(N) * s.reshape(S, DS)),
            "h": bf(np.random.standard_normal((B, D)) * s),
            "x2g": bf(np.random.standard_normal((B, D))),
            "w_g": bf(np.random.standard_normal((D, D)) / np.sqrt(D) / s),
            "b_g": bf(np.random.standard_normal(D) * 0.3),
            "bg": bf(1.0 + 0.1 * np.random.standard_normal(1))}


def core(a, vr, h, x2g, w_g, b_g, bg):
    hf = f64(h)
    hh = (f64(a).transpose(2, 0, 1) @ f64(vr).transpose(1, 0, 2)).transpose(1, 0, 2).reshape(B, D)
    h2g = (mxq(hf, 1, "e4m3") @ mxq(f64(w_g), 1, "e4m3").T) + f64(b_g)
    g = sigmoid(f64(x2g) + h2g + f64(bg))
    return g * hh + (1.0 - g) * hf


def e4m3fn_bytes(y):
    return np.clip(np.asarray(y, np.float64), -448.0, 448.0).astype(np.float32).astype(ml_dtypes.float8_e4m3fn).view(np.uint8)


def e4m3fn_values(b):
    return np.asarray(b, np.uint8).view(ml_dtypes.float8_e4m3fn).astype(np.float64)


def setup_inputs():
    d = draw0()
    x0 = np.asarray(d['w_g']).astype(np.float64)
    s = (np.max(np.abs(x0), axis=(0,), keepdims=True) / 448.0).astype(np.float32)
    out = {}
    for k, v in d.items():
        if k == 'w_g':
            out['w_g_bytes'] = e4m3fn_bytes(x0 / s.astype(np.float64))
            out['w_g_scale'] = s
        else:
            out[k] = v
    return out


def reference(a, vr, h, x2g, w_g_bytes, w_g_scale, b_g, bg):
    return core(a, vr, h, x2g, e4m3fn_values(w_g_bytes) * w_g_scale.astype(np.float64), b_g, bg)

@@ -1,0 +1,373 @@
+from contextlib import ExitStack
+
+import concourse.mybir as mybir
+from concourse.masks import make_identity
+
+B, D, S, N = 1024, 2048, 4, 128
+FLOPS = 2 * B * D * D + 2 * B * N * D
+
+F32 = mybir.dt.float32
+BF16 = mybir.dt.bfloat16
+U32 = mybir.dt.uint32
+U8 = mybir.dt.uint8
+FP8 = mybir.dt.float8_e4m3fn
+FP8X4 = mybir.dt.float8_e4m3fn_x4
+ADD = mybir.AluOpType.add
+SUB = mybir.AluOpType.subtract
+MULT = mybir.AluOpType.mult
+SIGMOID = mybir.ActivationFunctionType.Sigmoid
+
+P = 128
+OBW = 512
+NBT = B // P
+NOB = D // OBW
+NG = D // 512
+NR = OBW // P
+NT = NOB * NBT
+MANUAL = False
+LA = 10
+
+
+def o_on_gpsimd(t):
+    return t < NT - 2
+
+
+def folded(t):
+    return t < 22 or t % 2 == 0
+
+
+def xb_step(j):
+    return (4 * (j - LA)) // 3
+
+
+def tile_tpru_pb_kernel(tc, a, vr, h, x2g, w_g_bytes, w_g_scale, b_g, bg, out):
+    nc = tc.nc
+    with ExitStack() as ctx:
+        const = ctx.enter_context(tc.tile_pool(name="const", bufs=1))
+        wbf_pool = ctx.enter_context(tc.tile_pool(name="wbfp", bufs=4))
+        gh_pool = ctx.enter_context(tc.tile_pool(name="ghp", bufs=2))
+        wq_pool = ctx.enter_context(tc.tile_pool(name="wqp", bufs=2))
+        xb_pool = ctx.enter_context(tc.tile_pool(name="xbp", bufs=LA + 2))
+        wb_pool = ctx.enter_context(tc.tile_pool(name="wbp", bufs=6))
+        e_pool = ctx.enter_context(tc.tile_pool(name="ep", bufs=6))
+        d_pool = ctx.enter_context(tc.tile_pool(name="dsp", bufs=2))
+        tp_pool = ctx.enter_context(tc.psum_pool(name="tpp", bufs=3))
+        zp_pool = ctx.enter_context(tc.psum_pool(name="zpp", bufs=2))
+        dp_pool = ctx.enter_context(tc.psum_pool(name="dpp", bufs=3))
+        if MANUAL:
+            ctx.enter_context(tc.manual_schedule())
+
+        sc = const.tile([P, NG, 4], F32, name="sc")
+        bg_col = const.tile([P, 1], BF16, name="bg_col")
+        nc.scalar.dma_start(out=sc[:], in_=w_g_scale.rearrange("o (g p t) -> p (o g) t", p=P, t=4))
+        nc.scalar.dma_start(out=bg_col[:], in_=bg.partition_broadcast(P))
+        warm = const.tile([P, 1], F32, name="warm")
+        nc.vector.memset(warm[:], 0.0)
+        nc.scalar.activation(out=warm[:], in_=warm[:], func=SIGMOID)
+        ident = const.tile([P, P], F32, name="ident")
+        make_identity(nc, ident[:])
+        neg_ident = const.tile([P, P], BF16, name="neg_ident")
+        nc.vector.tensor_scalar(out=neg_ident[:], in0=ident[:], scalar1=-1.0, scalar2=None, op0=MULT)
+
+        wb = {}
+        h_sb = []
+        for bt in range(NBT):
+            h_tile = const.tile([P, D], BF16, name="h%d" % bt)
+            h_sb.append(h_tile)
+        x_sb = []
+        for i in range(2 * NOB):
+            x_tile = const.tile([P, NBT // 2, OBW], BF16, name="x%d" % i)
+            x_sb.append(x_tile)
+        bias_bf = const.tile([P, D], BF16, name="bias_bf")
+        a_raw = const.tile([P, NBT, N * S], BF16, name="a_raw")
+        vr_sb = const.tile([P, S, OBW], BF16, name="vr_sb")
+        aT = const.tile([P, S, B], BF16, name="aT")
+        hq = const.tile([P, NBT * 512], U32, name="hq", align_bytes=64)
+        hs = const.tile([P, NBT * 512], U8, name="hs", align_bytes=64)
+        gw = const.tile([P, NG, OBW, 4], BF16, name="gw", align_bytes=64)
+
+        w_rows = w_g_bytes.rearrange("(i p) k -> i p k", p=P)
+        h_rows = h.rearrange("(bt p) k -> bt p k", p=P)
+        x_blocks = x2g.rearrange("(bt p) (ob c) -> ob p bt c", p=P, c=OBW)
+
+        def load_w(i):
+            wb_new = wb_pool.tile([P, D], U8, name="wb")
+            wb[i] = wb_new
+            nc.sync.dma_start(out=wb_new[:], in_=w_rows[i])
+
+        def load_h(bt):
+            nc.sync.dma_start(out=h_sb[bt][:], in_=h_rows[bt])
+
+        def load_x(ob, half):
+            nc.sync.dma_start(out=x_sb[2 * ob + half][:], in_=x_blocks[ob][:, 4 * half : 4 * half + 4, :])
+
+        load_w(0)
+        load_w(1)
+        nc.sync.dma_start(out=bias_bf[:], in_=b_g.partition_broadcast(P))
+        load_x(0, 0)
+        load_w(2)
+        load_w(3)
+        load_h(0)
+        load_h(1)
+        load_x(0, 1)
+        nc.sync.dma_start(out=a_raw[:], in_=a.rearrange("(bt p) n s -> p bt (n s)", p=P))
+        nc.sync.dma_start(out=vr_sb[:], in_=vr)
+        load_w(NR)
+        load_h(2)
+        load_x(1, 0)
+        load_h(3)
+        load_w(NR + 1)
+        load_h(4)
+        load_x(1, 1)
+        load_w(NR + 2)
+        load_h(5)
+        load_h(6)
+        load_w(NR + 3)
+        load_h(7)
+
+        def word_transposes(src, pools):
+            words = src.bitcast(F32)
+            banks = []
+            for half in range(2):
+                bank = pools[half][0].tile([P, 512], F32, name=pools[half][1])
+                for g2 in range(2):
+                    g = 2 * half + g2
+                    for u in range(2):
+                        nc.tensor.transpose(
+                            bank[:, u * 256 + g2 * P : u * 256 + (g2 + 1) * P],
+                            words[:, 256 * g + u : 256 * (g + 1) : 2],
+                            ident[:],
+                        )
+                banks.append(bank)
+            return banks
+
+        TP2 = [(tp_pool, "tp"), (tp_pool, "tp")]
+        wbfs = {}
+
+        def w_cast_piece(nb, r, g):
+            if g == 0:
+                wbf_new = wbf_pool.tile([P, D], BF16, name="wbf")
+                wbfs[(nb, r)] = wbf_new
+            cols = slice(g * 512, (g + 1) * 512)
+            nc.scalar.copy(out=wbfs[(nb, r)][:, cols], in_=wb[nb * NR + r][:, cols].bitcast(FP8))
+
+        def w_scale(bank, r, half):
+            src = bank[:].bitcast(BF16).rearrange("p (u g r e) -> p g r u e", u=2, g=2, r=P, e=2)
+            dst = gw[:, 2 * half : 2 * half + 2, r * P : (r + 1) * P, :].rearrange("p g r (u e) -> p g r u e", u=2)
+            scl = (
+                sc[:, 2 * half : 2 * half + 2, :]
+                .rearrange("p g (u e) -> p g u e", u=2)
+                .unsqueeze(2)
+                .to_broadcast([P, 2, P, 2, 2])
+            )
+            nc.vector.tensor_tensor(out=dst, in0=src, in1=scl, op=MULT)
+
+        def w_quant_half(wq, ws, half):
+            cols = slice(half * 1024, (half + 1) * 1024)
+            nc.vector.quantize_mx(
+                out=wq[:, cols].bitcast(FP8X4),
+                scales=ws[:, cols],
+                in_=gw[:, 2 * half : 2 * half + 2, :, :].rearrange("p g o t -> p (g o t)"),
+            )
+
+        def new_wq():
+            wq = wq_pool.tile([P, NG * OBW], U32, name="wq", align_bytes=64)
+            ws = wq_pool.tile([P, NG * OBW], U8, name="ws", align_bytes=64)
+            return wq, ws
+
+        def h_copy(banks):
+            gh = gh_pool.tile([P, D], BF16, name="gh", align_bytes=64)
+            ghw = gh[:].bitcast(F32).rearrange("p (g r u) -> p g r u", g=NG, r=P, u=2)
+            for half in range(2):
+                nc.scalar.copy(
+                    out=ghw[:, 2 * half : 2 * half + 2, :, :],
+                    in_=banks[half][:].rearrange("p (u g r) -> p g r u", u=2, g=2, r=P),
+                )
+            return gh
+
+        def h_quant(bt, gh):
+            cols = slice(bt * 512, (bt + 1) * 512)
+            nc.vector.quantize_mx(out=hq[:, cols].bitcast(FP8X4), scales=hs[:, cols], in_=gh[:])
+
+        def a_transposes(pair, pool, name):
+            bank = pool.tile([P, 512], F32, name=name)
+            for j in range(2):
+                words = a_raw[:, 2 * pair + j, :].bitcast(F32)
+                for sp in range(2):
+                    nc.tensor.transpose(
+                        bank[:, (2 * j + sp) * P : (2 * j + sp + 1) * P], words[:, sp : 256 : 2], ident[:]
+                    )
+            return bank
+
+        def a_copy(pair, bank):
+            for j in range(2):
+                bt = 2 * pair + j
+                nc.scalar.copy(
+                    out=aT[:, :, bt * P : (bt + 1) * P].rearrange("n (sp e) b -> n sp e b", e=2),
+                    in_=bank[:, j * 256 : (j + 1) * 256].bitcast(BF16).rearrange("n (sp b e) -> n sp e b", sp=2, b=P, e=2),
+                )
+
+        def x_prep(t):
+            ob, bt = divmod(t, NBT)
+            xb = xb_pool.tile([P, OBW], F32, name="xb")
+            nc.gpsimd.tensor_tensor(
+                out=xb[:], in0=x_sb[2 * ob + bt // 4][:, bt % 4, :], in1=bias_bf[:, ob * OBW : (ob + 1) * OBW], op=ADD
+            )
+            return xb
+
+        def mm(t, wq, ws):
+            ob, bt = divmod(t, NBT)
+            zp = zp_pool.tile([P, OBW], F32, name="zp")
+            for g in range(NG):
+                hc = slice(bt * 512 + g * P, bt * 512 + (g + 1) * P)
+                wc = slice(g * OBW, (g + 1) * OBW)
+                nc.tensor.matmul_mx(
+                    out=zp[:],
+                    lhsT=hq[:, hc].bitcast(FP8X4),
+                    lhsT_scale=hs[:, hc],
+                    rhs=wq[:, wc].bitcast(FP8X4),
+                    rhs_scale=ws[:, wc],
+                    start=(g == 0),
+                    stop=(g == NG - 1),
+                )
+            fold = folded(t)
+            dp = dp_pool.tile([P, OBW], F32, name="dp")
+            nc.tensor.matmul(
+                out=dp[:], lhsT=aT[:, ob, bt * P : (bt + 1) * P], rhs=vr_sb[:, ob, :], start=True, stop=not fold
+            )
+            if fold:
+                nc.tensor.matmul(
+                    out=dp[:], lhsT=neg_ident[:], rhs=h_sb[bt][:, ob * OBW : (ob + 1) * OBW], start=False, stop=True
+                )
+            return zp, dp
+
+        def gate(t, zp, dp, xb):
+            ob, bt = divmod(t, NBT)
+            e = e_pool.tile([P, OBW], F32, name="e")
+            nc.vector.tensor_tensor(out=e[:], in0=zp[:], in1=xb[:], op=ADD)
+            nc.scalar.activation(out=e[:], in_=e[:], func=SIGMOID, bias=bg_col[:, 0:1])
+            if folded(t):
+                return e, dp
+            dsb = d_pool.tile([P, OBW], F32, name="dsb")
+            nc.vector.tensor_tensor(out=dsb[:], in0=dp[:], in1=h_sb[bt][:, ob * OBW : (ob + 1) * OBW], op=SUB)
+            return e, dsb
+
+        def blend(t, e, dd):
+            ob, bt = divmod(t, NBT)
+            h_cols = h_sb[bt][:, ob * OBW : (ob + 1) * OBW]
+            nc.vector.tensor_tensor(out=e[:], in0=e[:], in1=dd[:], op=MULT)
+            if o_on_gpsimd(t):
+                nc.gpsimd.tensor_tensor(out=e[:], in0=e[:], in1=h_cols, op=ADD)
+            else:
+                nc.vector.tensor_tensor(out=e[:], in0=e[:], in1=h_cols, op=ADD)
+            nc.sync.dma_start(out=out[bt * P : (bt + 1) * P, ob * OBW : (ob + 1) * OBW], in_=e[:])
+
+        run_at = {}
+        cast_at = {}
+        for nb in range(1, NOB):
+            for r in range(NR):
+                s_run = NBT * (nb - 1) + 2 * r - 1
+                run_at[s_run] = (nb, r)
+                cast_at.setdefault(s_run - 2, []).extend([(nb, r, 0), (nb, r, 1)])
+                cast_at.setdefault(s_run - 1, []).extend([(nb, r, 2), (nb, r, 3)])
+
+        def step_casts(s):
+            for nb, r, g in cast_at.get(s, []):
+                w_cast_piece(nb, r, g)
+
+        wbf0 = wbf_pool.tile([P, D], BF16, name="wbf")
+        wbfs[(0, 0)] = wbf0
+        nc.vector.tensor_copy(out=wbf0[:], in_=wb[0][:].bitcast(FP8))
+        for r in range(1, NR):
+            for g in range(NG):
+                w_cast_piece(0, r, g)
+        xbs = {}
+        for t in range(LA):
+            xbs[t] = x_prep(t)
+        xb_at = {}
+        for j in range(LA, NT):
+            xb_at.setdefault(xb_step(j), []).append(j)
+        load_at = {}
+        for nb in range(2, NOB):
+            for r in range(NR):
+                load_at.setdefault(NBT * (nb - 2) + 2 * r, []).append(("w", nb * NR + r, 0))
+            for half in range(2):
+                load_at.setdefault(NBT * (nb - 2) + 1 + 2 * half, []).append(("x", nb, half))
+
+        def w_run_head(r):
+            banks = word_transposes(wbfs[(0, r)][:], TP2)
+            w_scale(banks[0], r, 0)
+            w_scale(banks[1], r, 1)
+
+        w_run_head(0)
+        w_run_head(1)
+        hb0 = word_transposes(h_sb[0][:], [(zp_pool, "zp"), (zp_pool, "zp")])
+        gh0 = h_copy(hb0)
+        w_run_head(2)
+        hb1 = word_transposes(h_sb[1][:], [(dp_pool, "dp"), (dp_pool, "dp")])
+        gh1 = h_copy(hb1)
+        w_run_head(3)
+        ab0 = a_transposes(0, dp_pool, "dp")
+        a_copy(0, ab0)
+        step_casts(-3)
+        step_casts(-2)
+        step_casts(-1)
+        h_quant(0, gh0)
+        wq, ws = new_wq()
+        w_quant_half(wq, ws, 0)
+        w_quant_half(wq, ws, 1)
+        h_quant(1, gh1)
+        pend = word_transposes(wbfs[(1, 0)][:], TP2)
+        pend_r = 0
+        w_scale(pend[0], pend_r, 0)
+        cur = mm(0, wq, ws)
+        wq_next, ws_next = wq, ws
+
+        prev = None
+        for t in range(NT):
+            ob, bt = divmod(t, NBT)
+            nxt = None
+            if t + 1 < NT:
+                if (t + 1) % NBT == 0:
+                    wq, ws = wq_next, ws_next
+                nxt = mm(t + 1, wq, ws)
+            e, dd = gate(t, cur[0], cur[1], xbs[t])
+            hb = None
+            ab = None
+            if ob == 0 and bt + 2 < NBT:
+                hb = word_transposes(h_sb[bt + 2][:], TP2)
+                if bt % 2 == 0:
+                    ab = a_transposes((bt + 2) // 2, tp_pool, "tp")
+            new_run = None
+            if t in run_at:
+                new_run = word_transposes(wbfs[run_at[t]][:], TP2)
+            if prev is not None:
+                blend(prev[0], prev[1], prev[2])
+            prev = (t, e, dd)
+            gh = None
+            if hb is not None:
+                gh = h_copy(hb)
+            if ab is not None:
+                a_copy((bt + 2) // 2, ab)
+            if new_run is not None:
+                pend = new_run
+                pend_r = run_at[t][1]
+                w_scale(pend[0], pend_r, 0)
+            elif (t - 1) in run_at or t == 0:
+                w_scale(pend[1], pend_r, 1)
+            if gh is not None:
+                h_quant(bt + 2, gh)
+            step_casts(t)
+            if bt == 6 and ob + 1 < NOB:
+                wq_next, ws_next = new_wq()
+                w_quant_half(wq_next, ws_next, 0)
+                w_quant_half(wq_next, ws_next, 1)
+            for j in xb_at.get(t, []):
+                xbs[j] = x_prep(j)
+            for kind, i0, i1 in load_at.get(t, []):
+                if kind == "w":
+                    load_w(i0)
+                else:
+                    load_x(i0, i1)
+            cur = nxt
+        blend(prev[0], prev[1], prev[2])

@@ -78,9 +78,16 @@ def tile_tpru_pb_kernel(tc, a, vr, h, x2g, w_g_bytes, w_g_scale, b_g, bg, out):
         for i in range(2 * NOB):
             x_tile = const.tile([P, NBT // 2, OBW], BF16, name="x%d" % i)
             x_sb.append(x_tile)
-        bias_bf = const.tile([P, D], BF16, name="bias_bf")
-        a_raw = const.tile([P, NBT, N * S], BF16, name="a_raw")
-        vr_sb = const.tile([P, S, OBW], BF16, name="vr_sb")
+        bias_bf = []
+        vr_sb = []
+        a_raw = []
+        for i in range(NOB):
+            bias_tile = const.tile([P, OBW], BF16, name="bias%d" % i)
+            bias_bf.append(bias_tile)
+            vr_tile = const.tile([P, OBW], BF16, name="vr%d" % i)
+            vr_sb.append(vr_tile)
+            a_tile = const.tile([P, 2, N * S], BF16, name="a%d" % i)
+            a_raw.append(a_tile)
         aT = const.tile([P, S, B], BF16, name="aT")
         hq = const.tile([P, NBT * 512], U32, name="hq", align_bytes=64)
         hs = const.tile([P, NBT * 512], U8, name="hs", align_bytes=64)
@@ -101,29 +108,49 @@ def tile_tpru_pb_kernel(tc, a, vr, h, x2g, w_g_bytes, w_g_scale, b_g, bg, out):
         def load_x(ob, half):
             nc.sync.dma_start(out=x_sb[2 * ob + half][:], in_=x_blocks[ob][:, 4 * half : 4 * half + 4, :])
 
+        a_pairs = a.rearrange("(bt p) n s -> p bt (n s)", p=P)
+
+        def load_bias(ob):
+            nc.sync.dma_start(out=bias_bf[ob][:], in_=b_g[ob * OBW : (ob + 1) * OBW].partition_broadcast(P))
+
+        def load_a(pair):
+            nc.sync.dma_start(out=a_raw[pair][:], in_=a_pairs[:, 2 * pair : 2 * pair + 2, :])
+
+        def load_vr(ob):
+            nc.sync.dma_start(out=vr_sb[ob][:], in_=vr[:, ob, :])
+
         load_w(0)
         load_w(1)
-        nc.sync.dma_start(out=bias_bf[:], in_=b_g.partition_broadcast(P))
+        load_bias(0)
         load_x(0, 0)
         load_w(2)
         load_w(3)
         load_h(0)
+        load_a(0)
+        load_vr(0)
         load_h(1)
-        load_x(0, 1)
-        nc.sync.dma_start(out=a_raw[:], in_=a.rearrange("(bt p) n s -> p bt (n s)", p=P))
-        nc.sync.dma_start(out=vr_sb[:], in_=vr)
         load_w(NR)
+        load_x(0, 1)
         load_h(2)
+        load_a(1)
+        load_bias(1)
         load_x(1, 0)
         load_h(3)
         load_w(NR + 1)
         load_h(4)
-        load_x(1, 1)
+        load_a(2)
         load_w(NR + 2)
         load_h(5)
+        load_x(1, 1)
         load_h(6)
+        load_a(3)
         load_w(NR + 3)
         load_h(7)
+        load_vr(1)
+        load_bias(2)
+        load_vr(2)
+        load_bias(3)
+        load_vr(3)
 
         def word_transposes(src, pools):
             words = src.bitcast(F32)
@@ -192,7 +219,7 @@ def tile_tpru_pb_kernel(tc, a, vr, h, x2g, w_g_bytes, w_g_scale, b_g, bg, out):
         def a_transposes(pair, pool, name):
             bank = pool.tile([P, 512], F32, name=name)
             for j in range(2):
-                words = a_raw[:, 2 * pair + j, :].bitcast(F32)
+                words = a_raw[pair][:, j, :].bitcast(F32)
                 for sp in range(2):
                     nc.tensor.transpose(
                         bank[:, (2 * j + sp) * P : (2 * j + sp + 1) * P], words[:, sp : 256 : 2], ident[:]
@@ -211,7 +238,7 @@ def tile_tpru_pb_kernel(tc, a, vr, h, x2g, w_g_bytes, w_g_scale, b_g, bg, out):
             ob, bt = divmod(t, NBT)
             xb = xb_pool.tile([P, OBW], F32, name="xb")
             nc.gpsimd.tensor_tensor(
-                out=xb[:], in0=x_sb[2 * ob + bt // 4][:, bt % 4, :], in1=bias_bf[:, ob * OBW : (ob + 1) * OBW], op=ADD
+                out=xb[:], in0=x_sb[2 * ob + bt // 4][:, bt % 4, :], in1=bias_bf[ob][:], op=ADD
             )
             return xb
 
@@ -233,7 +260,7 @@ def tile_tpru_pb_kernel(tc, a, vr, h, x2g, w_g_bytes, w_g_scale, b_g, bg, out):
             fold = folded(t)
             dp = dp_pool.tile([P, OBW], F32, name="dp")
             nc.tensor.matmul(
-                out=dp[:], lhsT=aT[:, ob, bt * P : (bt + 1) * P], rhs=vr_sb[:, ob, :], start=True, stop=not fold
+                out=dp[:], lhsT=aT[:, ob, bt * P : (bt + 1) * P], rhs=vr_sb[ob][:], start=True, stop=not fold
             )
             if fold:
                 nc.tensor.matmul(

@@ -16,6 +16,7 @@ ADD = mybir.AluOpType.add
 SUB = mybir.AluOpType.subtract
 MULT = mybir.AluOpType.mult
 SIGMOID = mybir.ActivationFunctionType.Sigmoid
+COPY = mybir.ActivationFunctionType.Copy
 
 P = 128
 OBW = 512
@@ -26,6 +27,8 @@ NR = OBW // P
 NT = NOB * NBT
 MANUAL = False
 LA = 10
+S_BANKS = ((2, 0), (2, 2), (3, 1))
+S_RATE = 3
 
 
 def o_on_gpsimd(t):
@@ -188,6 +191,26 @@ def tile_tpru_pb_kernel(tc, a, vr, h, x2g, w_g_bytes, w_g_scale, b_g, bg, out):
                 .to_broadcast([P, 2, P, 2, 2])
             )
             nc.vector.tensor_tensor(out=dst, in0=src, in1=scl, op=MULT)
+
+        s_queue = []
+
+        def queue_scalar_scale(bank, r, half):
+            for g2 in range(2):
+                for u in range(2):
+                    for e2 in range(2):
+                        s_queue.append((bank, r, 2 * half + g2, g2, u, e2))
+
+        def emit_scalar_scale(n):
+            for i in range(min(n, len(s_queue))):
+                bank, r, g, g2, u, e2 = s_queue.pop(0)
+                src = bank[:].bitcast(BF16).rearrange("p (u g r e) -> p u g r e", u=2, g=2, r=P, e=2)
+                slot = 2 * u + e2
+                nc.scalar.activation(
+                    out=gw[:, g, r * P : (r + 1) * P, slot],
+                    in_=src[:, u, g2, :, e2],
+                    func=COPY,
+                    scale=sc[:, g, slot : slot + 1],
+                )
 
         def w_quant_half(wq, ws, half):
             cols = slice(half * 1024, (half + 1) * 1024)
@@ -381,11 +404,16 @@ def tile_tpru_pb_kernel(tc, a, vr, h, x2g, w_g_bytes, w_g_scale, b_g, bg, out):
                 pend_r = run_at[t][1]
                 w_scale(pend[0], pend_r, 0)
             elif (t - 1) in run_at or t == 0:
-                w_scale(pend[1], pend_r, 1)
+                if run_at.get(t - 1) in S_BANKS:
+                    queue_scalar_scale(pend[1], pend_r, 1)
+                else:
+                    w_scale(pend[1], pend_r, 1)
+            emit_scalar_scale(S_RATE)
             if gh is not None:
                 h_quant(bt + 2, gh)
             step_casts(t)
             if bt == 6 and ob + 1 < NOB:
+                assert len(s_queue) == 0
                 wq_next, ws_next = new_wq()
                 w_quant_half(wq_next, ws_next, 0)
                 w_quant_half(wq_next, ws_next, 1)

from contextlib import ExitStack

import concourse.mybir as mybir
from concourse.masks import make_identity

B, D, S, N = 1024, 2048, 4, 128
FLOPS = 2 * B * D * D + 2 * B * N * D

F32 = mybir.dt.float32
BF16 = mybir.dt.bfloat16
U32 = mybir.dt.uint32
U8 = mybir.dt.uint8
FP8 = mybir.dt.float8_e4m3fn
FP8X4 = mybir.dt.float8_e4m3fn_x4
ADD = mybir.AluOpType.add
SUB = mybir.AluOpType.subtract
MULT = mybir.AluOpType.mult
SIGMOID = mybir.ActivationFunctionType.Sigmoid
COPY = mybir.ActivationFunctionType.Copy

P = 128
OBW = 512
NBT = B // P
NOB = D // OBW
NG = D // 512
NR = OBW // P
NT = NOB * NBT
MANUAL = False
LA = 10
S_BANKS = ((2, 0), (2, 2), (3, 1))
S_RATE = 3


def o_on_gpsimd(t):
    return t < NT - 2


def folded(t):
    return t < 22 or t % 2 == 0


def xb_step(j):
    return (4 * (j - LA)) // 3


def tile_tpru_pb_kernel(tc, a, vr, h, x2g, w_g_bytes, w_g_scale, b_g, bg, out):
    nc = tc.nc
    with ExitStack() as ctx:
        const = ctx.enter_context(tc.tile_pool(name="const", bufs=1))
        wbf_pool = ctx.enter_context(tc.tile_pool(name="wbfp", bufs=4))
        gh_pool = ctx.enter_context(tc.tile_pool(name="ghp", bufs=2))
        wq_pool = ctx.enter_context(tc.tile_pool(name="wqp", bufs=2))
        xb_pool = ctx.enter_context(tc.tile_pool(name="xbp", bufs=LA + 2))
        wb_pool = ctx.enter_context(tc.tile_pool(name="wbp", bufs=6))
        e_pool = ctx.enter_context(tc.tile_pool(name="ep", bufs=6))
        d_pool = ctx.enter_context(tc.tile_pool(name="dsp", bufs=2))
        tp_pool = ctx.enter_context(tc.psum_pool(name="tpp", bufs=3))
        zp_pool = ctx.enter_context(tc.psum_pool(name="zpp", bufs=2))
        dp_pool = ctx.enter_context(tc.psum_pool(name="dpp", bufs=3))
        if MANUAL:
            ctx.enter_context(tc.manual_schedule())

        sc = const.tile([P, NG, 4], F32, name="sc")
        bg_col = const.tile([P, 1], BF16, name="bg_col")
        nc.scalar.dma_start(out=sc[:], in_=w_g_scale.rearrange("o (g p t) -> p (o g) t", p=P, t=4))
        nc.scalar.dma_start(out=bg_col[:], in_=bg.partition_broadcast(P))
        warm = const.tile([P, 1], F32, name="warm")
        nc.vector.memset(warm[:], 0.0)
        nc.scalar.activation(out=warm[:], in_=warm[:], func=SIGMOID)
        ident = const.tile([P, P], F32, name="ident")
        make_identity(nc, ident[:])
        neg_ident = const.tile([P, P], BF16, name="neg_ident")
        nc.vector.tensor_scalar(out=neg_ident[:], in0=ident[:], scalar1=-1.0, scalar2=None, op0=MULT)

        wb = {}
        h_sb = []
        for bt in range(NBT):
            h_tile = const.tile([P, D], BF16, name="h%d" % bt)
            h_sb.append(h_tile)
        x_sb = []
        for i in range(2 * NOB):
            x_tile = const.tile([P, NBT // 2, OBW], BF16, name="x%d" % i)
            x_sb.append(x_tile)
        bias_bf = []
        vr_sb = []
        a_raw = []
        for i in range(NOB):
            bias_tile = const.tile([P, OBW], BF16, name="bias%d" % i)
            bias_bf.append(bias_tile)
            vr_tile = const.tile([P, OBW], BF16, name="vr%d" % i)
            vr_sb.append(vr_tile)
            a_tile = const.tile([P, 2, N * S], BF16, name="a%d" % i)
            a_raw.append(a_tile)
        aT = const.tile([P, S, B], BF16, name="aT")
        hq = const.tile([P, NBT * 512], U32, name="hq", align_bytes=64)
        hs = const.tile([P, NBT * 512], U8, name="hs", align_bytes=64)
        gw = const.tile([P, NG, OBW, 4], BF16, name="gw", align_bytes=64)

        w_rows = w_g_bytes.rearrange("(i p) k -> i p k", p=P)
        h_rows = h.rearrange("(bt p) k -> bt p k", p=P)
        x_blocks = x2g.rearrange("(bt p) (ob c) -> ob p bt c", p=P, c=OBW)

        def load_w(i):
            wb_new = wb_pool.tile([P, D], U8, name="wb")
            wb[i] = wb_new
            nc.sync.dma_start(out=wb_new[:], in_=w_rows[i])

        def load_h(bt):
            nc.sync.dma_start(out=h_sb[bt][:], in_=h_rows[bt])

        def load_x(ob, half):
            nc.sync.dma_start(out=x_sb[2 * ob + half][:], in_=x_blocks[ob][:, 4 * half : 4 * half + 4, :])

        a_pairs = a.rearrange("(bt p) n s -> p bt (n s)", p=P)

        def load_bias(ob):
            nc.sync.dma_start(out=bias_bf[ob][:], in_=b_g[ob * OBW : (ob + 1) * OBW].partition_broadcast(P))

        def load_a(pair):
            nc.sync.dma_start(out=a_raw[pair][:], in_=a_pairs[:, 2 * pair : 2 * pair + 2, :])

        def load_vr(ob):
            nc.sync.dma_start(out=vr_sb[ob][:], in_=vr[:, ob, :])

        load_w(0)
        load_w(1)
        load_bias(0)
        load_x(0, 0)
        load_w(2)
        load_w(3)
        load_h(0)
        load_a(0)
        load_vr(0)
        load_h(1)
        load_w(NR)
        load_x(0, 1)
        load_h(2)
        load_a(1)
        load_bias(1)
        load_x(1, 0)
        load_h(3)
        load_w(NR + 1)
        load_h(4)
        load_a(2)
        load_w(NR + 2)
        load_h(5)
        load_x(1, 1)
        load_h(6)
        load_a(3)
        load_w(NR + 3)
        load_h(7)
        load_vr(1)
        load_bias(2)
        load_vr(2)
        load_bias(3)
        load_vr(3)

        def word_transposes(src, pools):
            words = src.bitcast(F32)
            banks = []
            for half in range(2):
                bank = pools[half][0].tile([P, 512], F32, name=pools[half][1])
                for g2 in range(2):
                    g = 2 * half + g2
                    for u in range(2):
                        nc.tensor.transpose(
                            bank[:, u * 256 + g2 * P : u * 256 + (g2 + 1) * P],
                            words[:, 256 * g + u : 256 * (g + 1) : 2],
                            ident[:],
                        )
                banks.append(bank)
            return banks

        TP2 = [(tp_pool, "tp"), (tp_pool, "tp")]
        wbfs = {}

        def w_cast_piece(nb, r, g):
            if g == 0:
                wbf_new = wbf_pool.tile([P, D], BF16, name="wbf")
                wbfs[(nb, r)] = wbf_new
            cols = slice(g * 512, (g + 1) * 512)
            nc.scalar.copy(out=wbfs[(nb, r)][:, cols], in_=wb[nb * NR + r][:, cols].bitcast(FP8))

        def w_scale(bank, r, half):
            src = bank[:].bitcast(BF16).rearrange("p (u g r e) -> p g r u e", u=2, g=2, r=P, e=2)
            dst = gw[:, 2 * half : 2 * half + 2, r * P : (r + 1) * P, :].rearrange("p g r (u e) -> p g r u e", u=2)
            scl = (
                sc[:, 2 * half : 2 * half + 2, :]
                .rearrange("p g (u e) -> p g u e", u=2)
                .unsqueeze(2)
                .to_broadcast([P, 2, P, 2, 2])
            )
            nc.vector.tensor_tensor(out=dst, in0=src, in1=scl, op=MULT)

        s_queue = []

        def queue_scalar_scale(bank, r, half):
            for g2 in range(2):
                for u in range(2):
                    for e2 in range(2):
                        s_queue.append((bank, r, 2 * half + g2, g2, u, e2))

        def emit_scalar_scale(n):
            for i in range(min(n, len(s_queue))):
                bank, r, g, g2, u, e2 = s_queue.pop(0)
                src = bank[:].bitcast(BF16).rearrange("p (u g r e) -> p u g r e", u=2, g=2, r=P, e=2)
                slot = 2 * u + e2
                nc.scalar.activation(
                    out=gw[:, g, r * P : (r + 1) * P, slot],
                    in_=src[:, u, g2, :, e2],
                    func=COPY,
                    scale=sc[:, g, slot : slot + 1],
                )

        def w_quant_half(wq, ws, half):
            cols = slice(half * 1024, (half + 1) * 1024)
            nc.vector.quantize_mx(
                out=wq[:, cols].bitcast(FP8X4),
                scales=ws[:, cols],
                in_=gw[:, 2 * half : 2 * half + 2, :, :].rearrange("p g o t -> p (g o t)"),
            )

        def new_wq():
            wq = wq_pool.tile([P, NG * OBW], U32, name="wq", align_bytes=64)
            ws = wq_pool.tile([P, NG * OBW], U8, name="ws", align_bytes=64)
            return wq, ws

        def h_copy(banks):
            gh = gh_pool.tile([P, D], BF16, name="gh", align_bytes=64)
            ghw = gh[:].bitcast(F32).rearrange("p (g r u) -> p g r u", g=NG, r=P, u=2)
            for half in range(2):
                nc.scalar.copy(
                    out=ghw[:, 2 * half : 2 * half + 2, :, :],
                    in_=banks[half][:].rearrange("p (u g r) -> p g r u", u=2, g=2, r=P),
                )
            return gh

        def h_quant(bt, gh):
            cols = slice(bt * 512, (bt + 1) * 512)
            nc.vector.quantize_mx(out=hq[:, cols].bitcast(FP8X4), scales=hs[:, cols], in_=gh[:])

        def a_transposes(pair, pool, name):
            bank = pool.tile([P, 512], F32, name=name)
            for j in range(2):
                words = a_raw[pair][:, j, :].bitcast(F32)
                for sp in range(2):
                    nc.tensor.transpose(
                        bank[:, (2 * j + sp) * P : (2 * j + sp + 1) * P], words[:, sp : 256 : 2], ident[:]
                    )
            return bank

        def a_copy(pair, bank):
            for j in range(2):
                bt = 2 * pair + j
                nc.scalar.copy(
                    out=aT[:, :, bt * P : (bt + 1) * P].rearrange("n (sp e) b -> n sp e b", e=2),
                    in_=bank[:, j * 256 : (j + 1) * 256].bitcast(BF16).rearrange("n (sp b e) -> n sp e b", sp=2, b=P, e=2),
                )

        def x_prep(t):
            ob, bt = divmod(t, NBT)
            xb = xb_pool.tile([P, OBW], F32, name="xb")
            nc.gpsimd.tensor_tensor(
                out=xb[:], in0=x_sb[2 * ob + bt // 4][:, bt % 4, :], in1=bias_bf[ob][:], op=ADD
            )
            return xb

        def mm(t, wq, ws):
            ob, bt = divmod(t, NBT)
            zp = zp_pool.tile([P, OBW], F32, name="zp")
            for g in range(NG):
                hc = slice(bt * 512 + g * P, bt * 512 + (g + 1) * P)
                wc = slice(g * OBW, (g + 1) * OBW)
                nc.tensor.matmul_mx(
                    out=zp[:],
                    lhsT=hq[:, hc].bitcast(FP8X4),
                    lhsT_scale=hs[:, hc],
                    rhs=wq[:, wc].bitcast(FP8X4),
                    rhs_scale=ws[:, wc],
                    start=(g == 0),
                    stop=(g == NG - 1),
                )
            fold = folded(t)
            dp = dp_pool.tile([P, OBW], F32, name="dp")
            nc.tensor.matmul(
                out=dp[:], lhsT=aT[:, ob, bt * P : (bt + 1) * P], rhs=vr_sb[ob][:], start=True, stop=not fold
            )
            if fold:
                nc.tensor.matmul(
                    out=dp[:], lhsT=neg_ident[:], rhs=h_sb[bt][:, ob * OBW : (ob + 1) * OBW], start=False, stop=True
                )
            return zp, dp

        def gate(t, zp, dp, xb):
            ob, bt = divmod(t, NBT)
            e = e_pool.tile([P, OBW], F32, name="e")
            nc.vector.tensor_tensor(out=e[:], in0=zp[:], in1=xb[:], op=ADD)
            nc.scalar.activation(out=e[:], in_=e[:], func=SIGMOID, bias=bg_col[:, 0:1])
            if folded(t):
                return e, dp
            dsb = d_pool.tile([P, OBW], F32, name="dsb")
            nc.vector.tensor_tensor(out=dsb[:], in0=dp[:], in1=h_sb[bt][:, ob * OBW : (ob + 1) * OBW], op=SUB)
            return e, dsb

        def blend(t, e, dd):
            ob, bt = divmod(t, NBT)
            h_cols = h_sb[bt][:, ob * OBW : (ob + 1) * OBW]
            nc.vector.tensor_tensor(out=e[:], in0=e[:], in1=dd[:], op=MULT)
            if o_on_gpsimd(t):
                nc.gpsimd.tensor_tensor(out=e[:], in0=e[:], in1=h_cols, op=ADD)
            else:
                nc.vector.tensor_tensor(out=e[:], in0=e[:], in1=h_cols, op=ADD)
            nc.sync.dma_start(out=out[bt * P : (bt + 1) * P, ob * OBW : (ob + 1) * OBW], in_=e[:])

        run_at = {}
        cast_at = {}
        for nb in range(1, NOB):
            for r in range(NR):
                s_run = NBT * (nb - 1) + 2 * r - 1
                run_at[s_run] = (nb, r)
                cast_at.setdefault(s_run - 2, []).extend([(nb, r, 0), (nb, r, 1)])
                cast_at.setdefault(s_run - 1, []).extend([(nb, r, 2), (nb, r, 3)])

        def step_casts(s):
            for nb, r, g in cast_at.get(s, []):
                w_cast_piece(nb, r, g)

        wbf0 = wbf_pool.tile([P, D], BF16, name="wbf")
        wbfs[(0, 0)] = wbf0
        nc.vector.tensor_copy(out=wbf0[:], in_=wb[0][:].bitcast(FP8))
        for r in range(1, NR):
            for g in range(NG):
                w_cast_piece(0, r, g)
        xbs = {}
        for t in range(LA):
            xbs[t] = x_prep(t)
        xb_at = {}
        for j in range(LA, NT):
            xb_at.setdefault(xb_step(j), []).append(j)
        load_at = {}
        for nb in range(2, NOB):
            for r in range(NR):
                load_at.setdefault(NBT * (nb - 2) + 2 * r, []).append(("w", nb * NR + r, 0))
            for half in range(2):
                load_at.setdefault(NBT * (nb - 2) + 1 + 2 * half, []).append(("x", nb, half))

        def w_run_head(r):
            banks = word_transposes(wbfs[(0, r)][:], TP2)
            w_scale(banks[0], r, 0)
            w_scale(banks[1], r, 1)

        w_run_head(0)
        w_run_head(1)
        hb0 = word_transposes(h_sb[0][:], [(zp_pool, "zp"), (zp_pool, "zp")])
        gh0 = h_copy(hb0)
        w_run_head(2)
        hb1 = word_transposes(h_sb[1][:], [(dp_pool, "dp"), (dp_pool, "dp")])
        gh1 = h_copy(hb1)
        w_run_head(3)
        ab0 = a_transposes(0, dp_pool, "dp")
        a_copy(0, ab0)
        step_casts(-3)
        step_casts(-2)
        step_casts(-1)
        h_quant(0, gh0)
        wq, ws = new_wq()
        w_quant_half(wq, ws, 0)
        w_quant_half(wq, ws, 1)
        h_quant(1, gh1)
        pend = word_transposes(wbfs[(1, 0)][:], TP2)
        pend_r = 0
        w_scale(pend[0], pend_r, 0)
        cur = mm(0, wq, ws)
        wq_next, ws_next = wq, ws

        prev = None
        for t in range(NT):
            ob, bt = divmod(t, NBT)
            nxt = None
            if t + 1 < NT:
                if (t + 1) % NBT == 0:
                    wq, ws = wq_next, ws_next
                nxt = mm(t + 1, wq, ws)
            e, dd = gate(t, cur[0], cur[1], xbs[t])
            hb = None
            ab = None
            if ob == 0 and bt + 2 < NBT:
                hb = word_transposes(h_sb[bt + 2][:], TP2)
                if bt % 2 == 0:
                    ab = a_transposes((bt + 2) // 2, tp_pool, "tp")
            new_run = None
            if t in run_at:
                new_run = word_transposes(wbfs[run_at[t]][:], TP2)
            if prev is not None:
                blend(prev[0], prev[1], prev[2])
            prev = (t, e, dd)
            gh = None
            if hb is not None:
                gh = h_copy(hb)
            if ab is not None:
                a_copy((bt + 2) // 2, ab)
            if new_run is not None:
                pend = new_run
                pend_r = run_at[t][1]
                w_scale(pend[0], pend_r, 0)
            elif (t - 1) in run_at or t == 0:
                if run_at.get(t - 1) in S_BANKS:
                    queue_scalar_scale(pend[1], pend_r, 1)
                else:
                    w_scale(pend[1], pend_r, 1)
            emit_scalar_scale(S_RATE)
            if gh is not None:
                h_quant(bt + 2, gh)
            step_casts(t)
            if bt == 6 and ob + 1 < NOB:
                assert len(s_queue) == 0
                wq_next, ws_next = new_wq()
                w_quant_half(wq_next, ws_next, 0)
                w_quant_half(wq_next, ws_next, 1)
            for j in xb_at.get(t, []):
                xbs[j] = x_prep(j)
            for kind, i0, i1 in load_at.get(t, []):
                if kind == "w":
                    load_w(i0)
                else:
                    load_x(i0, i1)
            cur = nxt
        blend(prev[0], prev[1], prev[2])
